import numpy as np
import ml_dtypes

BF16 = ml_dtypes.bfloat16


def bf(x):
    return np.asarray(x, np.float32).astype(BF16)


def f32(x):
    return np.asarray(x, np.float32)


def f64(x):
    return np.asarray(x).astype(np.float64)


def striped(idx):
    return np.tile(idx.reshape(-1, 16).T, (8, 1))


C, HD, HALF, S, N = 256, 128, 64, 2048, 512


def rope_table():
    inv_freq = 1.0 / 10000 ** (np.arange(0, HD, 2) / HD)
    freqs = np.einsum('i,j->ij', np.arange(S), inv_freq).astype('float32')
    emb = np.concatenate((freqs, freqs), axis=-1)
    both = np.concatenate((np.sin(emb), np.cos(emb)), axis=-1)
    return f32(np.ascontiguousarray(both.T)).reshape(C, S)


def rope(a, tab, idx):
    sin = tab[:HD][:, idx]
    cos = tab[HD:][:, idx]
    rot = np.concatenate((-a[HALF:], a[:HALF]), axis=0)
    return a * cos + rot * sin


def setup_inputs():
    return {"tab": rope_table(), "q": f32(np.random.standard_normal((HD, N))), "k": f32(np.random.standard_normal((HD, N))), "v": bf(2.0 * np.random.standard_normal((N, HD))), "offs": striped(np.random.permutation(S)[:N])}


def reference(tab, q, k, v, offs):
    idx = offs[:16].T.reshape(-1)
    t = f64(tab)
    qr = rope(f64(q), t, idx)
    kr = rope(f64(k), t, idx)
    sc = qr.T @ kr / np.sqrt(HD)
    keep = np.tril(np.ones((N, N), dtype=bool))
    sc = np.where(keep, sc, -np.inf)
    e = np.exp(sc - sc.max(axis=1, keepdims=True))
    att = e / e.sum(axis=1, keepdims=True)
    return (att @ f64(v)).T

@@ -1,0 +1,134 @@
+import math
+from contextlib import ExitStack
+
+import concourse.mybir as mybir
+from concourse.masks import make_identity
+
+F32 = mybir.dt.float32
+BF16 = mybir.dt.bfloat16
+U16 = mybir.dt.uint16
+I32 = mybir.dt.int32
+MULT = mybir.AluOpType.mult
+ADD = mybir.AluOpType.add
+IS_GT = mybir.AluOpType.is_gt
+IS_LT = mybir.AluOpType.is_lt
+EXP = mybir.ActivationFunctionType.Exp
+COPY = mybir.ActivationFunctionType.Copy
+X = mybir.AxisListType.X
+
+P = 128
+HALF = 64
+S = 2048
+N = 512
+NB = N // P
+V_PITCH = 144
+MASKED = -1.0e30
+
+FLOPS = 2 * P * N * (N + 1)
+
+
+def block(b):
+    return slice(b * P, (b + 1) * P)
+
+
+def tile_flaxllamaattention_kernel(tc, tab, q, k, v, offs, out):
+    nc = tc.nc
+    with ExitStack() as ctx:
+        held = ctx.enter_context(tc.tile_pool(name="held", bufs=1))
+        work = ctx.enter_context(tc.tile_pool(name="work", bufs=2))
+        psum_a = ctx.enter_context(tc.psum_pool(name="psum_a", bufs=2))
+        psum_b = ctx.enter_context(tc.psum_pool(name="psum_b", bufs=2))
+        psum_o = ctx.enter_context(tc.psum_pool(name="psum_o", bufs=2))
+
+        offsets = held.tile([P, N // 16], U16, name="offsets")
+        nc.sync.dma_start(offsets[:], offs)
+        rk = held.tile([P, N], F32, name="rk")
+        rq = held.tile([P, N], F32, name="rq")
+        for rotated, plain in ((rk, k), (rq, q)):
+            nc.sync.dma_start(rotated[0:HALF, :], plain[HALF:P, :])
+            nc.sync.dma_start(rotated[HALF:P, :], plain[0:HALF, :])
+        sin_tab = held.tile([P, S], F32, name="sin_tab")
+        nc.sync.dma_start(sin_tab[:], tab[0:P, :])
+        cos_tab = held.tile([P, S], F32, name="cos_tab")
+        nc.sync.dma_start(cos_tab[:], tab[P : 2 * P, :])
+        k_sb = held.tile([P, N], F32, name="k_sb")
+        nc.sync.dma_start(k_sb[:], k)
+        q_sb = held.tile([P, N], F32, name="q_sb")
+        nc.sync.dma_start(q_sb[:], q)
+        v_ones = held.tile([P, NB, V_PITCH], BF16, name="v_ones")
+        nc.sync.dma_start(v_ones[:, :, 0:P], v.rearrange("(b t) d -> t b d", t=P))
+        nc.vector.memset(v_ones[:, :, P : P + 1], 1.0)
+
+        ident_bf = held.tile([P, P], BF16, name="ident_bf")
+        make_identity(nc, ident_bf[:])
+        ident_f32 = held.tile([P, P], F32, name="ident_f32")
+        make_identity(nc, ident_f32[:])
+        ones_bf = held.tile([P, P], BF16, name="ones_bf")
+        nc.gpsimd.memset(ones_bf[:], 1.0)
+        col_minus_row = held.tile([P, P], I32, name="col_minus_row")
+        nc.gpsimd.iota(col_minus_row[:], pattern=[[1, P]], base=0, channel_multiplier=-1)
+        mask_jt = held.tile([P, P], BF16, name="mask_jt")
+        nc.vector.tensor_scalar(out=mask_jt[:], in0=col_minus_row[:], scalar1=0.0, scalar2=MASKED,
+                                op0=IS_GT, op1=MULT)
+        mask_tj = held.tile([P, P], BF16, name="mask_tj")
+        nc.vector.tensor_scalar(out=mask_tj[:], in0=col_minus_row[:], scalar1=0.0, scalar2=MASKED,
+                                op0=IS_LT, op1=MULT)
+
+        for rotated in (rk, rq):
+            nc.vector.tensor_scalar(
+                out=rotated[0:HALF, :], in0=rotated[0:HALF, :],
+                scalar1=-1.0, scalar2=None, op0=MULT,
+            )
+        k_sin = held.tile([P, N], F32, name="k_sin")
+        nc.vector.tensor_tensor(k_sin[:], sin_tab[:].indirect(offsets[:]), rk[:], MULT)
+        q_sin = held.tile([P, N], F32, name="q_sin")
+        nc.vector.tensor_tensor(q_sin[:], sin_tab[:].indirect(offsets[:]), rq[:], MULT)
+        k_cos = held.tile([P, N], F32, name="k_cos")
+        nc.vector.tensor_tensor(k_cos[:], cos_tab[:].indirect(offsets[:]), k_sb[:], MULT)
+        kr = held.tile([P, N], BF16, name="kr")
+        nc.vector.tensor_tensor(kr[:], k_cos[:], k_sin[:], ADD)
+        q_cos = held.tile([P, N], F32, name="q_cos")
+        nc.vector.tensor_tensor(q_cos[:], cos_tab[:].indirect(offsets[:]), q_sb[:], MULT)
+        qr = held.tile([P, N], BF16, name="qr")
+        nc.vector.tensor_tensor(qr[:], q_cos[:], q_sin[:], ADD)
+
+        out_sb = held.tile([P, N], F32, name="out_sb")
+        for jb in range(NB):
+            seen = (jb + 1) * P
+
+            s_jt = psum_a.tile([P, N], F32, name="s_jt")
+            nc.tensor.matmul(s_jt[:, 0:seen], lhsT=qr[:, block(jb)], rhs=kr[:, 0:seen],
+                             start=True, stop=False)
+            nc.tensor.matmul(s_jt[:, block(jb)], lhsT=ident_bf[:], rhs=mask_jt[:],
+                             start=False, stop=True)
+            neg_max = work.tile([P, 1], F32, name="neg_max")
+            nc.vector.reduce_max(neg_max[:], s_jt[:, 0:seen], axis=X, negate=True)
+            diag = work.tile([P, P], BF16, name="diag")
+            nc.vector.tensor_scalar(out=diag[:], in0=ident_bf[:], scalar1=neg_max[:, 0:1],
+                                    scalar2=None, op0=MULT)
+
+            s_tj = psum_b.tile([P, N], F32, name="s_tj")
+            for tb in range(jb + 1):
+                nc.tensor.matmul(s_tj[:, block(tb)], lhsT=kr[:, block(tb)], rhs=qr[:, block(jb)],
+                                 start=(tb == 0), stop=False)
+            nc.tensor.matmul(s_tj[:, block(jb)], lhsT=ident_bf[:], rhs=mask_tj[:],
+                             start=False, stop=False)
+            for tb in range(jb + 1):
+                nc.tensor.matmul(s_tj[:, block(tb)], lhsT=ones_bf[:], rhs=diag[:],
+                                 start=False, stop=(tb == jb))
+            e_tj = work.tile([P, N], BF16, name="e_tj")
+            nc.scalar.activation(e_tj[:, 0:seen], s_tj[:, 0:seen], EXP, scale=1.0 / math.sqrt(P))
+
+            o_jd = psum_o.tile([P, P + 1], F32, name="o_jd")
+            for tb in range(jb + 1):
+                nc.tensor.matmul(o_jd[:], lhsT=e_tj[:, block(tb)], rhs=v_ones[:, tb, 0 : P + 1],
+                                 start=(tb == 0), stop=(tb == jb))
+            r_sum = work.tile([P, 1], F32, name="r_sum")
+            nc.vector.reciprocal(r_sum[:], o_jd[:, P : P + 1])
+            o_norm = work.tile([P, P], F32, name="o_norm")
+            nc.scalar.activation(o_norm[:], o_jd[:, 0:P], COPY, scale=r_sum[:, 0:1])
+
+            o_dj = psum_o.tile([P, P], F32, name="o_dj")
+            nc.tensor.transpose(o_dj[:], o_norm[:], ident_f32[:])
+            nc.vector.tensor_copy(out_sb[:, block(jb)], o_dj[:])
+            nc.sync.dma_start(out[:, block(jb)], out_sb[:, block(jb)])

@@ -21,6 +21,7 @@ HALF = 64
 S = 2048
 N = 512
 NB = N // P
+PIECE = 256
 V_PITCH = 144
 MASKED = -1.0e30
 
@@ -63,8 +64,6 @@ def tile_flaxllamaattention_kernel(tc, tab, q, k, v, offs, out):
         make_identity(nc, ident_bf[:])
         ident_f32 = held.tile([P, P], F32, name="ident_f32")
         make_identity(nc, ident_f32[:])
-        ones_bf = held.tile([P, P], BF16, name="ones_bf")
-        nc.gpsimd.memset(ones_bf[:], 1.0)
         col_minus_row = held.tile([P, P], I32, name="col_minus_row")
         nc.gpsimd.iota(col_minus_row[:], pattern=[[1, P]], base=0, channel_multiplier=-1)
         mask_jt = held.tile([P, P], BF16, name="mask_jt")
@@ -83,17 +82,24 @@ def tile_flaxllamaattention_kernel(tc, tab, q, k, v, offs, out):
         nc.vector.tensor_tensor(k_sin[:], sin_tab[:].indirect(offsets[:]), rk[:], MULT)
         q_sin = held.tile([P, N], F32, name="q_sin")
         nc.vector.tensor_tensor(q_sin[:], sin_tab[:].indirect(offsets[:]), rq[:], MULT)
+        warm = psum_a.tile([P, N], F32, name="warm", tag="s_jt")
+        for product in (k_sin, q_sin):
+            nc.tensor.matmul(warm[:], lhsT=ident_f32[:], rhs=product[:], start=True, stop=True)
+
         k_cos = held.tile([P, N], F32, name="k_cos")
         nc.vector.tensor_tensor(k_cos[:], cos_tab[:].indirect(offsets[:]), k_sb[:], MULT)
         kr = held.tile([P, N], BF16, name="kr")
         nc.vector.tensor_tensor(kr[:], k_cos[:], k_sin[:], ADD)
         q_cos = held.tile([P, N], F32, name="q_cos")
-        nc.vector.tensor_tensor(q_cos[:], cos_tab[:].indirect(offsets[:]), q_sb[:], MULT)
         qr = held.tile([P, N], BF16, name="qr")
-        nc.vector.tensor_tensor(qr[:], q_cos[:], q_sin[:], ADD)
+        for piece in reversed(range(N // PIECE)):
+            cols = slice(piece * PIECE, (piece + 1) * PIECE)
+            picked = cos_tab[:].indirect(offsets[:, piece * (PIECE // 16) : (piece + 1) * (PIECE // 16)])
+            nc.vector.tensor_tensor(q_cos[:, cols], picked, q_sb[:, cols], MULT)
+            nc.vector.tensor_tensor(qr[:, cols], q_cos[:, cols], q_sin[:, cols], ADD)
 
         out_sb = held.tile([P, N], F32, name="out_sb")
-        for jb in range(NB):
+        for jb in reversed(range(NB)):
             seen = (jb + 1) * P
 
             s_jt = psum_a.tile([P, N], F32, name="s_jt")
@@ -101,11 +107,9 @@ def tile_flaxllamaattention_kernel(tc, tab, q, k, v, offs, out):
                              start=True, stop=False)
             nc.tensor.matmul(s_jt[:, block(jb)], lhsT=ident_bf[:], rhs=mask_jt[:],
                              start=False, stop=True)
-            neg_max = work.tile([P, 1], F32, name="neg_max")
-            nc.vector.reduce_max(neg_max[:], s_jt[:, 0:seen], axis=X, negate=True)
-            diag = work.tile([P, P], BF16, name="diag")
-            nc.vector.tensor_scalar(out=diag[:], in0=ident_bf[:], scalar1=neg_max[:, 0:1],
-                                    scalar2=None, op0=MULT)
+            neg_max = work.tile([P, 1], BF16, name="neg_max")
+            with nc.allow_low_precision(reason="any shift near the maximum serves: it cancels in the division"):
+                nc.vector.reduce_max(neg_max[:], s_jt[:, 0:seen], axis=X, negate=True)
 
             s_tj = psum_b.tile([P, N], F32, name="s_tj")
             for tb in range(jb + 1):
@@ -113,9 +117,10 @@ def tile_flaxllamaattention_kernel(tc, tab, q, k, v, offs, out):
                                  start=(tb == 0), stop=False)
             nc.tensor.matmul(s_tj[:, block(jb)], lhsT=ident_bf[:], rhs=mask_tj[:],
                              start=False, stop=False)
-            for tb in range(jb + 1):
-                nc.tensor.matmul(s_tj[:, block(tb)], lhsT=ones_bf[:], rhs=diag[:],
-                                 start=False, stop=(tb == jb))
+            nc.tensor.matmul(s_tj[:, 0:seen].rearrange("t (b j) -> t b j", j=P),
+                             lhsT=neg_max[:, 0:1].to_broadcast([P, P]),
+                             rhs=ident_bf[:].unsqueeze(1).to_broadcast([P, jb + 1, P]),
+                             start=False, stop=True)
             e_tj = work.tile([P, N], BF16, name="e_tj")
             nc.scalar.activation(e_tj[:, 0:seen], s_tj[:, 0:seen], EXP, scale=1.0 / math.sqrt(P))
 

@@ -49,9 +49,11 @@ def tile_flaxllamaattention_kernel(tc, tab, q, k, v, offs, out):
             nc.sync.dma_start(rotated[0:HALF, :], plain[HALF:P, :])
             nc.sync.dma_start(rotated[HALF:P, :], plain[0:HALF, :])
         sin_tab = held.tile([P, S], F32, name="sin_tab")
-        nc.sync.dma_start(sin_tab[:], tab[0:P, :])
+        for c in range(0, S, N):
+            nc.sync.dma_start(sin_tab[:, c : c + N], tab[0:P, c : c + N])
         cos_tab = held.tile([P, S], F32, name="cos_tab")
-        nc.sync.dma_start(cos_tab[:], tab[P : 2 * P, :])
+        for c in range(0, S, N):
+            nc.sync.dma_start(cos_tab[:, c : c + N], tab[P : 2 * P, c : c + N])
         k_sb = held.tile([P, N], F32, name="k_sb")
         nc.sync.dma_start(k_sb[:], k)
         q_sb = held.tile([P, N], F32, name="q_sb")

@@ -47,13 +47,11 @@ def tile_flaxllamaattention_kernel(tc, tab, q, k, v, offs, out):
         rq = held.tile([P, N], F32, name="rq")
         for rotated, plain in ((rk, k), (rq, q)):
             nc.sync.dma_start(rotated[0:HALF, :], plain[HALF:P, :])
-            nc.sync.dma_start(rotated[HALF:P, :], plain[0:HALF, :])
+            nc.scalar.dma_start(rotated[HALF:P, :], plain[0:HALF, :])
         sin_tab = held.tile([P, S], F32, name="sin_tab")
-        for c in range(0, S, N):
-            nc.sync.dma_start(sin_tab[:, c : c + N], tab[0:P, c : c + N])
+        nc.sync.dma_start(sin_tab[:], tab[0:P, :])
         cos_tab = held.tile([P, S], F32, name="cos_tab")
-        for c in range(0, S, N):
-            nc.sync.dma_start(cos_tab[:, c : c + N], tab[P : 2 * P, c : c + N])
+        nc.sync.dma_start(cos_tab[:], tab[P : 2 * P, :])
         k_sb = held.tile([P, N], F32, name="k_sb")
         nc.sync.dma_start(k_sb[:], k)
         q_sb = held.tile([P, N], F32, name="q_sb")

@@ -47,7 +47,7 @@ def tile_flaxllamaattention_kernel(tc, tab, q, k, v, offs, out):
         rq = held.tile([P, N], F32, name="rq")
         for rotated, plain in ((rk, k), (rq, q)):
             nc.sync.dma_start(rotated[0:HALF, :], plain[HALF:P, :])
-            nc.scalar.dma_start(rotated[HALF:P, :], plain[0:HALF, :])
+            nc.sync.dma_start(rotated[HALF:P, :], plain[0:HALF, :])
         sin_tab = held.tile([P, S], F32, name="sin_tab")
         nc.sync.dma_start(sin_tab[:], tab[0:P, :])
         cos_tab = held.tile([P, S], F32, name="cos_tab")
@@ -82,10 +82,6 @@ def tile_flaxllamaattention_kernel(tc, tab, q, k, v, offs, out):
         nc.vector.tensor_tensor(k_sin[:], sin_tab[:].indirect(offsets[:]), rk[:], MULT)
         q_sin = held.tile([P, N], F32, name="q_sin")
         nc.vector.tensor_tensor(q_sin[:], sin_tab[:].indirect(offsets[:]), rq[:], MULT)
-        warm = psum_a.tile([P, N], F32, name="warm", tag="s_jt")
-        for product in (k_sin, q_sin):
-            nc.tensor.matmul(warm[:], lhsT=ident_f32[:], rhs=product[:], start=True, stop=True)
-
         k_cos = held.tile([P, N], F32, name="k_cos")
         nc.vector.tensor_tensor(k_cos[:], cos_tab[:].indirect(offsets[:]), k_sb[:], MULT)
         kr = held.tile([P, N], BF16, name="kr")

@@ -82,17 +82,21 @@ def tile_flaxllamaattention_kernel(tc, tab, q, k, v, offs, out):
         nc.vector.tensor_tensor(k_sin[:], sin_tab[:].indirect(offsets[:]), rk[:], MULT)
         q_sin = held.tile([P, N], F32, name="q_sin")
         nc.vector.tensor_tensor(q_sin[:], sin_tab[:].indirect(offsets[:]), rq[:], MULT)
+        warm = psum_a.tile([P, N], F32, name="warm", tag="s_jt")
+        for product in (k_sin, q_sin):
+            nc.tensor.matmul(warm[:], lhsT=ident_f32[:], rhs=product[:], start=True, stop=True)
+
         k_cos = held.tile([P, N], F32, name="k_cos")
         nc.vector.tensor_tensor(k_cos[:], cos_tab[:].indirect(offsets[:]), k_sb[:], MULT)
         kr = held.tile([P, N], BF16, name="kr")
         nc.vector.tensor_tensor(kr[:], k_cos[:], k_sin[:], ADD)
         q_cos = held.tile([P, N], F32, name="q_cos")
         qr = held.tile([P, N], BF16, name="qr")
-        for piece in reversed(range(N // PIECE)):
+        for piece, adder in ((1, nc.vector), (0, nc.gpsimd)):
             cols = slice(piece * PIECE, (piece + 1) * PIECE)
             picked = cos_tab[:].indirect(offsets[:, piece * (PIECE // 16) : (piece + 1) * (PIECE // 16)])
             nc.vector.tensor_tensor(q_cos[:, cols], picked, q_sb[:, cols], MULT)
-            nc.vector.tensor_tensor(qr[:, cols], q_cos[:, cols], q_sin[:, cols], ADD)
+            adder.tensor_tensor(qr[:, cols], q_cos[:, cols], q_sin[:, cols], ADD)
 
         out_sb = held.tile([P, N], F32, name="out_sb")
         for jb in reversed(range(NB)):

@@ -13,7 +13,6 @@ ADD = mybir.AluOpType.add
 IS_GT = mybir.AluOpType.is_gt
 IS_LT = mybir.AluOpType.is_lt
 EXP = mybir.ActivationFunctionType.Exp
-COPY = mybir.ActivationFunctionType.Copy
 X = mybir.AxisListType.X
 
 P = 128
@@ -131,7 +130,7 @@ def tile_flaxllamaattention_kernel(tc, tab, q, k, v, offs, out):
             r_sum = work.tile([P, 1], F32, name="r_sum")
             nc.vector.reciprocal(r_sum[:], o_jd[:, P : P + 1])
             o_norm = work.tile([P, P], F32, name="o_norm")
-            nc.scalar.activation(o_norm[:], o_jd[:, 0:P], COPY, scale=r_sum[:, 0:1])
+            nc.vector.tensor_scalar(out=o_norm[:], in0=o_jd[:, 0:P], scalar1=r_sum[:, 0:1], scalar2=None, op0=MULT)
 
             o_dj = psum_o.tile([P, P], F32, name="o_dj")
             nc.tensor.transpose(o_dj[:], o_norm[:], ident_f32[:])

@@ -121,7 +121,9 @@ def tile_flaxllamaattention_kernel(tc, tab, q, k, v, offs, out):
                              rhs=ident_bf[:].unsqueeze(1).to_broadcast([P, jb + 1, P]),
                              start=False, stop=True)
             e_tj = work.tile([P, N], BF16, name="e_tj")
-            nc.scalar.activation(e_tj[:, 0:seen], s_tj[:, 0:seen], EXP, scale=1.0 / math.sqrt(P))
+            for lo in range(0, seen, 2 * P):
+                hi = min(lo + 2 * P, seen)
+                nc.scalar.activation(e_tj[:, lo:hi], s_tj[:, lo:hi], EXP, scale=1.0 / math.sqrt(P))
 
             o_jd = psum_o.tile([P, P + 1], F32, name="o_jd")
             for tb in range(jb + 1):

@@ -20,7 +20,6 @@ HALF = 64
 S = 2048
 N = 512
 NB = N // P
-PIECE = 256
 V_PITCH = 144
 MASKED = -1.0e30
 
@@ -82,8 +81,8 @@ def tile_flaxllamaattention_kernel(tc, tab, q, k, v, offs, out):
         q_sin = held.tile([P, N], F32, name="q_sin")
         nc.vector.tensor_tensor(q_sin[:], sin_tab[:].indirect(offsets[:]), rq[:], MULT)
         warm = psum_a.tile([P, N], F32, name="warm", tag="s_jt")
-        for product in (k_sin, q_sin):
-            nc.tensor.matmul(warm[:], lhsT=ident_f32[:], rhs=product[:], start=True, stop=True)
+        nc.tensor.matmul(warm[:], lhsT=ident_f32[:], rhs=k_sin[:], start=True, stop=True)
+        nc.tensor.matmul(warm[:, 0 : N // 2], lhsT=ident_f32[:], rhs=q_sin[:, 0 : N // 2], start=True, stop=True)
 
         k_cos = held.tile([P, N], F32, name="k_cos")
         nc.vector.tensor_tensor(k_cos[:], cos_tab[:].indirect(offsets[:]), k_sb[:], MULT)
@@ -91,11 +90,11 @@ def tile_flaxllamaattention_kernel(tc, tab, q, k, v, offs, out):
         nc.vector.tensor_tensor(kr[:], k_cos[:], k_sin[:], ADD)
         q_cos = held.tile([P, N], F32, name="q_cos")
         qr = held.tile([P, N], BF16, name="qr")
-        for piece, adder in ((1, nc.vector), (0, nc.gpsimd)):
-            cols = slice(piece * PIECE, (piece + 1) * PIECE)
-            picked = cos_tab[:].indirect(offsets[:, piece * (PIECE // 16) : (piece + 1) * (PIECE // 16)])
-            nc.vector.tensor_tensor(q_cos[:, cols], picked, q_sb[:, cols], MULT)
-            adder.tensor_tensor(qr[:, cols], q_cos[:, cols], q_sin[:, cols], ADD)
+        for jb in reversed(range(NB)):
+            picked = cos_tab[:].indirect(offsets[:, jb * (P // 16) : (jb + 1) * (P // 16)])
+            nc.vector.tensor_tensor(q_cos[:, block(jb)], picked, q_sb[:, block(jb)], MULT)
+            adder = nc.vector if jb >= NB // 2 else nc.gpsimd
+            adder.tensor_tensor(qr[:, block(jb)], q_cos[:, block(jb)], q_sin[:, block(jb)], ADD)
 
         out_sb = held.tile([P, N], F32, name="out_sb")
         for jb in reversed(range(NB)):
@@ -121,9 +120,8 @@ def tile_flaxllamaattention_kernel(tc, tab, q, k, v, offs, out):
                              rhs=ident_bf[:].unsqueeze(1).to_broadcast([P, jb + 1, P]),
                              start=False, stop=True)
             e_tj = work.tile([P, N], BF16, name="e_tj")
-            for lo in range(0, seen, 2 * P):
-                hi = min(lo + 2 * P, seen)
-                nc.scalar.activation(e_tj[:, lo:hi], s_tj[:, lo:hi], EXP, scale=1.0 / math.sqrt(P))
+            for tb in range(jb + 1):
+                nc.scalar.activation(e_tj[:, block(tb)], s_tj[:, block(tb)], EXP, scale=1.0 / math.sqrt(P))
 
             o_jd = psum_o.tile([P, P + 1], F32, name="o_jd")
             for tb in range(jb + 1):

@@ -101,9 +101,12 @@ def tile_flaxllamaattention_kernel(tc, tab, q, k, v, offs, out):
             seen = (jb + 1) * P
 
             s_jt = psum_a.tile([P, N], F32, name="s_jt")
-            nc.tensor.matmul(s_jt[:, 0:seen], lhsT=qr[:, block(jb)], rhs=kr[:, 0:seen],
-                             start=True, stop=False)
             nc.tensor.matmul(s_jt[:, block(jb)], lhsT=ident_bf[:], rhs=mask_jt[:],
+                             start=True, stop=False)
+            if jb > 0:
+                nc.tensor.matmul(s_jt[:, 0 : jb * P], lhsT=qr[:, block(jb)], rhs=kr[:, 0 : jb * P],
+                                 start=False, stop=False)
+            nc.tensor.matmul(s_jt[:, block(jb)], lhsT=qr[:, block(jb)], rhs=kr[:, block(jb)],
                              start=False, stop=True)
             neg_max = work.tile([P, 1], BF16, name="neg_max")
             with nc.allow_low_precision(reason="any shift near the maximum serves: it cancels in the division"):

@@ -7,11 +7,10 @@ from concourse.masks import make_identity
 F32 = mybir.dt.float32
 BF16 = mybir.dt.bfloat16
 U16 = mybir.dt.uint16
-I32 = mybir.dt.int32
 MULT = mybir.AluOpType.mult
 ADD = mybir.AluOpType.add
-IS_GT = mybir.AluOpType.is_gt
-IS_LT = mybir.AluOpType.is_lt
+NOT_EQUAL = mybir.AluOpType.not_equal
+IS_GE = mybir.AluOpType.is_ge
 EXP = mybir.ActivationFunctionType.Exp
 X = mybir.AxisListType.X
 
@@ -41,19 +40,15 @@ def tile_flaxllamaattention_kernel(tc, tab, q, k, v, offs, out):
 
         offsets = held.tile([P, N // 16], U16, name="offsets")
         nc.sync.dma_start(offsets[:], offs)
-        rk = held.tile([P, N], F32, name="rk")
-        rq = held.tile([P, N], F32, name="rq")
-        for rotated, plain in ((rk, k), (rq, q)):
-            nc.sync.dma_start(rotated[0:HALF, :], plain[HALF:P, :])
-            nc.sync.dma_start(rotated[HALF:P, :], plain[0:HALF, :])
-        sin_tab = held.tile([P, S], F32, name="sin_tab")
-        nc.sync.dma_start(sin_tab[:], tab[0:P, :])
-        cos_tab = held.tile([P, S], F32, name="cos_tab")
-        nc.sync.dma_start(cos_tab[:], tab[P : 2 * P, :])
         k_sb = held.tile([P, N], F32, name="k_sb")
         nc.sync.dma_start(k_sb[:], k)
+        sin_tab = held.tile([P, S], F32, name="sin_tab")
+        nc.sync.dma_start(sin_tab[0:HALF, :], tab[HALF:P, :])
+        nc.sync.dma_start(sin_tab[HALF:P, :], tab[0:HALF, :])
         q_sb = held.tile([P, N], F32, name="q_sb")
         nc.sync.dma_start(q_sb[:], q)
+        cos_tab = held.tile([P, S], F32, name="cos_tab")
+        nc.sync.dma_start(cos_tab[:], tab[P : 2 * P, :])
         v_ones = held.tile([P, NB, V_PITCH], BF16, name="v_ones")
         nc.sync.dma_start(v_ones[:, :, 0:P], v.rearrange("(b t) d -> t b d", t=P))
         nc.vector.memset(v_ones[:, :, P : P + 1], 1.0)
@@ -62,39 +57,39 @@ def tile_flaxllamaattention_kernel(tc, tab, q, k, v, offs, out):
         make_identity(nc, ident_bf[:])
         ident_f32 = held.tile([P, P], F32, name="ident_f32")
         make_identity(nc, ident_f32[:])
-        col_minus_row = held.tile([P, P], I32, name="col_minus_row")
-        nc.gpsimd.iota(col_minus_row[:], pattern=[[1, P]], base=0, channel_multiplier=-1)
+        rotate = held.tile([P, P], F32, name="rotate")
+        nc.gpsimd.memset(rotate[:], 0.0)
+        for shift, sign in ((HALF, -1.0), (-HALF, 1.0)):
+            nc.gpsimd.affine_select(out=rotate[:], in_=rotate[:], compare_op=NOT_EQUAL, fill=sign,
+                                    base=-shift, pattern=[[-1, P]], channel_multiplier=1)
         mask_jt = held.tile([P, P], BF16, name="mask_jt")
-        nc.vector.tensor_scalar(out=mask_jt[:], in0=col_minus_row[:], scalar1=0.0, scalar2=MASKED,
-                                op0=IS_GT, op1=MULT)
         mask_tj = held.tile([P, P], BF16, name="mask_tj")
-        nc.vector.tensor_scalar(out=mask_tj[:], in0=col_minus_row[:], scalar1=0.0, scalar2=MASKED,
-                                op0=IS_LT, op1=MULT)
+        for mask, col_step in ((mask_jt, -1), (mask_tj, 1)):
+            nc.gpsimd.memset(mask[:], 0.0)
+            nc.gpsimd.affine_select(out=mask[:], in_=mask[:], compare_op=IS_GE, fill=MASKED,
+                                    base=0, pattern=[[col_step, P]], channel_multiplier=-col_step)
 
-        for rotated in (rk, rq):
-            nc.vector.tensor_scalar(
-                out=rotated[0:HALF, :], in0=rotated[0:HALF, :],
-                scalar1=-1.0, scalar2=None, op0=MULT,
-            )
         k_sin = held.tile([P, N], F32, name="k_sin")
-        nc.vector.tensor_tensor(k_sin[:], sin_tab[:].indirect(offsets[:]), rk[:], MULT)
         q_sin = held.tile([P, N], F32, name="q_sin")
-        nc.vector.tensor_tensor(q_sin[:], sin_tab[:].indirect(offsets[:]), rq[:], MULT)
-        warm = psum_a.tile([P, N], F32, name="warm", tag="s_jt")
-        nc.tensor.matmul(warm[:], lhsT=ident_f32[:], rhs=k_sin[:], start=True, stop=True)
-        nc.tensor.matmul(warm[:, 0 : N // 2], lhsT=ident_f32[:], rhs=q_sin[:, 0 : N // 2], start=True, stop=True)
+        rk_sin = psum_o.tile([P, N], F32, name="rk_sin", tag="o_dj")
+        rq_sin = psum_o.tile([P, N], F32, name="rq_sin", tag="o_dj")
+        for product, rotated, plain, halves in ((k_sin, rk_sin, k_sb, (0, 1)), (q_sin, rq_sin, q_sb, (1, 0))):
+            for h in halves:
+                tokens = slice(h * N // 2, (h + 1) * N // 2)
+                picked = sin_tab[:].indirect(offsets[:, h * N // 32 : (h + 1) * N // 32])
+                nc.vector.tensor_tensor(product[:, tokens], picked, plain[:, tokens], MULT)
+                nc.tensor.matmul(rotated[:, tokens], lhsT=rotate[:], rhs=product[:, tokens], start=True, stop=True)
 
         k_cos = held.tile([P, N], F32, name="k_cos")
         nc.vector.tensor_tensor(k_cos[:], cos_tab[:].indirect(offsets[:]), k_sb[:], MULT)
         kr = held.tile([P, N], BF16, name="kr")
-        nc.vector.tensor_tensor(kr[:], k_cos[:], k_sin[:], ADD)
+        nc.vector.tensor_tensor(kr[:], k_cos[:], rk_sin[:], ADD)
         q_cos = held.tile([P, N], F32, name="q_cos")
         qr = held.tile([P, N], BF16, name="qr")
         for jb in reversed(range(NB)):
             picked = cos_tab[:].indirect(offsets[:, jb * (P // 16) : (jb + 1) * (P // 16)])
             nc.vector.tensor_tensor(q_cos[:, block(jb)], picked, q_sb[:, block(jb)], MULT)
-            adder = nc.vector if jb >= NB // 2 else nc.gpsimd
-            adder.tensor_tensor(qr[:, block(jb)], q_cos[:, block(jb)], q_sin[:, block(jb)], ADD)
+            nc.vector.tensor_tensor(qr[:, block(jb)], q_cos[:, block(jb)], rq_sin[:, block(jb)], ADD)
 
         out_sb = held.tile([P, N], F32, name="out_sb")
         for jb in reversed(range(NB)):

@@ -41,14 +41,13 @@ def tile_flaxllamaattention_kernel(tc, tab, q, k, v, offs, out):
         offsets = held.tile([P, N // 16], U16, name="offsets")
         nc.sync.dma_start(offsets[:], offs)
         k_sb = held.tile([P, N], F32, name="k_sb")
-        nc.sync.dma_start(k_sb[:], k)
         sin_tab = held.tile([P, S], F32, name="sin_tab")
-        nc.sync.dma_start(sin_tab[0:HALF, :], tab[HALF:P, :])
-        nc.sync.dma_start(sin_tab[HALF:P, :], tab[0:HALF, :])
         q_sb = held.tile([P, N], F32, name="q_sb")
-        nc.sync.dma_start(q_sb[:], q)
         cos_tab = held.tile([P, S], F32, name="cos_tab")
-        nc.sync.dma_start(cos_tab[:], tab[P : 2 * P, :])
+        sines, cosines = tab[0:P, :], tab[P : 2 * P, :]
+        for tile, rows, lower_at in ((k_sb, k, 0), (sin_tab, sines, 1), (q_sb, q, 0), (cos_tab, cosines, 0)):
+            nc.sync.dma_start(tile[lower_at:P:2, :], rows[0:HALF, :])
+            nc.sync.dma_start(tile[1 - lower_at : P : 2, :], rows[HALF:P, :])
         v_ones = held.tile([P, NB, V_PITCH], BF16, name="v_ones")
         nc.sync.dma_start(v_ones[:, :, 0:P], v.rearrange("(b t) d -> t b d", t=P))
         nc.vector.memset(v_ones[:, :, P : P + 1], 1.0)
@@ -59,9 +58,9 @@ def tile_flaxllamaattention_kernel(tc, tab, q, k, v, offs, out):
         make_identity(nc, ident_f32[:])
         rotate = held.tile([P, P], F32, name="rotate")
         nc.gpsimd.memset(rotate[:], 0.0)
-        for shift, sign in ((HALF, -1.0), (-HALF, 1.0)):
+        for base, h_step, sign in ((-1, 2 * P, -1.0), (2 * P, -2 * P, 1.0)):
             nc.gpsimd.affine_select(out=rotate[:], in_=rotate[:], compare_op=NOT_EQUAL, fill=sign,
-                                    base=-shift, pattern=[[-1, P]], channel_multiplier=1)
+                                    base=base, pattern=[[-2, HALF], [h_step, 2]], channel_multiplier=1)
         mask_jt = held.tile([P, P], BF16, name="mask_jt")
         mask_tj = held.tile([P, P], BF16, name="mask_tj")
         for mask, col_step in ((mask_jt, -1), (mask_tj, 1)):

@@ -9,17 +9,17 @@ BF16 = mybir.dt.bfloat16
 U16 = mybir.dt.uint16
 MULT = mybir.AluOpType.mult
 ADD = mybir.AluOpType.add
+MIN = mybir.AluOpType.min
 NOT_EQUAL = mybir.AluOpType.not_equal
 IS_GE = mybir.AluOpType.is_ge
 EXP = mybir.ActivationFunctionType.Exp
-X = mybir.AxisListType.X
 
 P = 128
 HALF = 64
 S = 2048
 N = 512
 NB = N // P
-V_PITCH = 144
+SCALE = 1.0 / math.sqrt(P)
 MASKED = -1.0e30
 
 FLOPS = 2 * P * N * (N + 1)
@@ -33,10 +33,9 @@ def tile_flaxllamaattention_kernel(tc, tab, q, k, v, offs, out):
     nc = tc.nc
     with ExitStack() as ctx:
         held = ctx.enter_context(tc.tile_pool(name="held", bufs=1))
-        work = ctx.enter_context(tc.tile_pool(name="work", bufs=2))
-        psum_a = ctx.enter_context(tc.psum_pool(name="psum_a", bufs=2))
-        psum_b = ctx.enter_context(tc.psum_pool(name="psum_b", bufs=2))
-        psum_o = ctx.enter_context(tc.psum_pool(name="psum_o", bufs=2))
+        work = ctx.enter_context(tc.tile_pool(name="work", bufs=4))
+        psum_s = ctx.enter_context(tc.psum_pool(name="psum_s", bufs=NB))
+        psum_o = ctx.enter_context(tc.psum_pool(name="psum_o", bufs=NB))
 
         offsets = held.tile([P, N // 16], U16, name="offsets")
         nc.sync.dma_start(offsets[:], offs)
@@ -48,9 +47,8 @@ def tile_flaxllamaattention_kernel(tc, tab, q, k, v, offs, out):
         for tile, rows, lower_at in ((k_sb, k, 0), (sin_tab, sines, 1), (q_sb, q, 0), (cos_tab, cosines, 0)):
             nc.sync.dma_start(tile[lower_at:P:2, :], rows[0:HALF, :])
             nc.sync.dma_start(tile[1 - lower_at : P : 2, :], rows[HALF:P, :])
-        v_ones = held.tile([P, NB, V_PITCH], BF16, name="v_ones")
-        nc.sync.dma_start(v_ones[:, :, 0:P], v.rearrange("(b t) d -> t b d", t=P))
-        nc.vector.memset(v_ones[:, :, P : P + 1], 1.0)
+        v_sb = held.tile([P, NB, P], BF16, name="v_sb")
+        nc.sync.dma_start(v_sb[:], v.rearrange("(b t) d -> t b d", t=P))
 
         ident_bf = held.tile([P, P], BF16, name="ident_bf")
         make_identity(nc, ident_bf[:])
@@ -62,27 +60,34 @@ def tile_flaxllamaattention_kernel(tc, tab, q, k, v, offs, out):
             nc.gpsimd.affine_select(out=rotate[:], in_=rotate[:], compare_op=NOT_EQUAL, fill=sign,
                                     base=base, pattern=[[-2, HALF], [h_step, 2]], channel_multiplier=1)
         mask_jt = held.tile([P, P], BF16, name="mask_jt")
-        mask_tj = held.tile([P, P], BF16, name="mask_tj")
-        for mask, col_step in ((mask_jt, -1), (mask_tj, 1)):
-            nc.gpsimd.memset(mask[:], 0.0)
-            nc.gpsimd.affine_select(out=mask[:], in_=mask[:], compare_op=IS_GE, fill=MASKED,
-                                    base=0, pattern=[[col_step, P]], channel_multiplier=-col_step)
+        nc.gpsimd.memset(mask_jt[:], 0.0)
+        nc.gpsimd.affine_select(out=mask_jt[:], in_=mask_jt[:], compare_op=IS_GE, fill=MASKED,
+                                base=0, pattern=[[-1, P]], channel_multiplier=1)
 
+        warm_k = psum_o.tile([P, N], F32, name="warm_k", tag="o_dj")
+        nc.tensor.matmul(warm_k[:], lhsT=ident_f32[:], rhs=k_sb[:], start=True, stop=True)
+
+        half = [slice(0, N // 2), slice(N // 2, N)]
+        picks = [offsets[:, 0 : N // 32], offsets[:, N // 32 : N // 16]]
         k_sin = held.tile([P, N], F32, name="k_sin")
+        kr_sum = psum_o.tile([P, N // 2], F32, name="kr_sum", tag="o_dj")
+        rk_sin = psum_o.tile([P, N // 2], F32, name="rk_sin", tag="o_dj")
+        for h, rotated in ((0, kr_sum), (1, rk_sin)):
+            nc.vector.tensor_tensor(k_sin[:, half[h]], sin_tab[:].indirect(picks[h]), k_sb[:, half[h]], MULT)
+            nc.tensor.matmul(rotated[:], lhsT=rotate[:], rhs=k_sin[:, half[h]], start=True, stop=(h == 1))
         q_sin = held.tile([P, N], F32, name="q_sin")
-        rk_sin = psum_o.tile([P, N], F32, name="rk_sin", tag="o_dj")
         rq_sin = psum_o.tile([P, N], F32, name="rq_sin", tag="o_dj")
-        for product, rotated, plain, halves in ((k_sin, rk_sin, k_sb, (0, 1)), (q_sin, rq_sin, q_sb, (1, 0))):
-            for h in halves:
-                tokens = slice(h * N // 2, (h + 1) * N // 2)
-                picked = sin_tab[:].indirect(offsets[:, h * N // 32 : (h + 1) * N // 32])
-                nc.vector.tensor_tensor(product[:, tokens], picked, plain[:, tokens], MULT)
-                nc.tensor.matmul(rotated[:, tokens], lhsT=rotate[:], rhs=product[:, tokens], start=True, stop=True)
+        for h in (1, 0):
+            nc.vector.tensor_tensor(q_sin[:, half[h]], sin_tab[:].indirect(picks[h]), q_sb[:, half[h]], MULT)
+            nc.tensor.matmul(rq_sin[:, half[h]], lhsT=rotate[:], rhs=q_sin[:, half[h]], start=True, stop=True)
 
         k_cos = held.tile([P, N], F32, name="k_cos")
-        nc.vector.tensor_tensor(k_cos[:], cos_tab[:].indirect(offsets[:]), k_sb[:], MULT)
         kr = held.tile([P, N], BF16, name="kr")
-        nc.vector.tensor_tensor(kr[:], k_cos[:], rk_sin[:], ADD)
+        for h in (0, 1):
+            nc.vector.tensor_tensor(k_cos[:, half[h]], cos_tab[:].indirect(picks[h]), k_sb[:, half[h]], MULT)
+        nc.tensor.matmul(kr_sum[:], lhsT=ident_f32[:], rhs=k_cos[:, half[0]], start=False, stop=True)
+        nc.scalar.copy(kr[:, half[0]], kr_sum[:])
+        nc.vector.tensor_tensor(kr[:, half[1]], k_cos[:, half[1]], rk_sin[:], ADD)
         q_cos = held.tile([P, N], F32, name="q_cos")
         qr = held.tile([P, N], BF16, name="qr")
         for jb in reversed(range(NB)):
@@ -90,11 +95,11 @@ def tile_flaxllamaattention_kernel(tc, tab, q, k, v, offs, out):
             nc.vector.tensor_tensor(q_cos[:, block(jb)], picked, q_sb[:, block(jb)], MULT)
             nc.vector.tensor_tensor(qr[:, block(jb)], q_cos[:, block(jb)], rq_sin[:, block(jb)], ADD)
 
-        out_sb = held.tile([P, N], F32, name="out_sb")
+        att = {}
         for jb in reversed(range(NB)):
             seen = (jb + 1) * P
 
-            s_jt = psum_a.tile([P, N], F32, name="s_jt")
+            s_jt = psum_s.tile([P, N], F32, name="s_jt")
             nc.tensor.matmul(s_jt[:, block(jb)], lhsT=ident_bf[:], rhs=mask_jt[:],
                              start=True, stop=False)
             if jb > 0:
@@ -102,34 +107,35 @@ def tile_flaxllamaattention_kernel(tc, tab, q, k, v, offs, out):
                                  start=False, stop=False)
             nc.tensor.matmul(s_jt[:, block(jb)], lhsT=qr[:, block(jb)], rhs=kr[:, block(jb)],
                              start=False, stop=True)
-            neg_max = work.tile([P, 1], BF16, name="neg_max")
-            with nc.allow_low_precision(reason="any shift near the maximum serves: it cancels in the division"):
-                nc.vector.reduce_max(neg_max[:], s_jt[:, 0:seen], axis=X, negate=True)
 
-            s_tj = psum_b.tile([P, N], F32, name="s_tj")
-            for tb in range(jb + 1):
-                nc.tensor.matmul(s_tj[:, block(tb)], lhsT=kr[:, block(tb)], rhs=qr[:, block(jb)],
-                                 start=(tb == 0), stop=False)
-            nc.tensor.matmul(s_tj[:, block(jb)], lhsT=ident_bf[:], rhs=mask_tj[:],
-                             start=False, stop=False)
-            nc.tensor.matmul(s_tj[:, 0:seen].rearrange("t (b j) -> t b j", j=P),
-                             lhsT=neg_max[:, 0:1].to_broadcast([P, P]),
-                             rhs=ident_bf[:].unsqueeze(1).to_broadcast([P, jb + 1, P]),
-                             start=False, stop=True)
-            e_tj = work.tile([P, N], BF16, name="e_tj")
-            for tb in range(jb + 1):
-                nc.scalar.activation(e_tj[:, block(tb)], s_tj[:, block(tb)], EXP, scale=1.0 / math.sqrt(P))
-
-            o_jd = psum_o.tile([P, P + 1], F32, name="o_jd")
-            for tb in range(jb + 1):
-                nc.tensor.matmul(o_jd[:], lhsT=e_tj[:, block(tb)], rhs=v_ones[:, tb, 0 : P + 1],
-                                 start=(tb == 0), stop=(tb == jb))
+            neg_s = work.tile([P, N], F32, name="neg_s")
+            bias = work.tile([P, 1], F32, name="bias")
+            nc.vector.tensor_scalar(out=neg_s[:, 0:seen], in0=s_jt[:, 0:seen], scalar1=-SCALE, scalar2=None,
+                                    op0=MULT, op1=MIN, accum_out=bias[:])
+            if jb == NB - 1:
+                warm = psum_o.tile([P, N // 2], F32, name="warm", tag="o_dj")
+                nc.tensor.matmul(warm[:], lhsT=rotate[:], rhs=neg_s[:, 0 : N // 2], start=True, stop=True)
+            e_jt = work.tile([P, N], F32, name="e_jt")
+            e_sum = work.tile([P, 1], F32, name="e_sum")
+            nc.scalar.activation(e_jt[:, 0:seen], neg_s[:, 0:seen], EXP, bias=bias[:], scale=-1.0,
+                                 accum_out=e_sum[:])
             r_sum = work.tile([P, 1], F32, name="r_sum")
-            nc.vector.reciprocal(r_sum[:], o_jd[:, P : P + 1])
-            o_norm = work.tile([P, P], F32, name="o_norm")
-            nc.vector.tensor_scalar(out=o_norm[:], in0=o_jd[:, 0:P], scalar1=r_sum[:, 0:1], scalar2=None, op0=MULT)
+            nc.vector.reciprocal(r_sum[:], e_sum[:])
+            att[jb] = work.tile([P, N], BF16, name="att")
+            nc.vector.tensor_scalar(out=att[jb][:, 0:seen], in0=e_jt[:, 0:seen], scalar1=r_sum[:, 0:1], scalar2=None,
+                                    op0=MULT)
 
+        out_sb = held.tile([P, N], F32, name="out_sb")
+        for jb in reversed(range(NB)):
+            seen = (jb + 1) * P
+            att_t = psum_s.tile([P, N], BF16, name="att_t", tag="s_jt")
+            for tb in range(jb + 1):
+                nc.tensor.transpose(att_t[:, block(tb)], att[jb][:, block(tb)], ident_bf[:])
+            att_tj = work.tile([P, N], BF16, name="att_tj")
+            nc.vector.tensor_copy(att_tj[:, 0:seen], att_t[:, 0:seen])
             o_dj = psum_o.tile([P, P], F32, name="o_dj")
-            nc.tensor.transpose(o_dj[:], o_norm[:], ident_f32[:])
-            nc.vector.tensor_copy(out_sb[:, block(jb)], o_dj[:])
+            for tb in range(jb + 1):
+                nc.tensor.matmul(o_dj[:], lhsT=v_sb[:, tb, :], rhs=att_tj[:, block(tb)],
+                                 start=(tb == 0), stop=(tb == jb))
+            nc.scalar.copy(out_sb[:, block(jb)], o_dj[:])
             nc.sync.dma_start(out[:, block(jb)], out_sb[:, block(jb)])

@@ -80,6 +80,8 @@ def tile_flaxllamaattention_kernel(tc, tab, q, k, v, offs, out):
         for h in (1, 0):
             nc.vector.tensor_tensor(q_sin[:, half[h]], sin_tab[:].indirect(picks[h]), q_sb[:, half[h]], MULT)
             nc.tensor.matmul(rq_sin[:, half[h]], lhsT=rotate[:], rhs=q_sin[:, half[h]], start=True, stop=True)
+        rq_sin_early = held.tile([P, N // 2], F32, name="rq_sin_early")
+        nc.scalar.copy(rq_sin_early[:], rq_sin[:, half[0]])
 
         k_cos = held.tile([P, N], F32, name="k_cos")
         kr = held.tile([P, N], BF16, name="kr")
@@ -93,7 +95,8 @@ def tile_flaxllamaattention_kernel(tc, tab, q, k, v, offs, out):
         for jb in reversed(range(NB)):
             picked = cos_tab[:].indirect(offsets[:, jb * (P // 16) : (jb + 1) * (P // 16)])
             nc.vector.tensor_tensor(q_cos[:, block(jb)], picked, q_sb[:, block(jb)], MULT)
-            nc.vector.tensor_tensor(qr[:, block(jb)], q_cos[:, block(jb)], rq_sin[:, block(jb)], ADD)
+            adder, rotated = (nc.vector, rq_sin) if jb >= NB // 2 else (nc.gpsimd, rq_sin_early)
+            adder.tensor_tensor(qr[:, block(jb)], q_cos[:, block(jb)], rotated[:, block(jb)], ADD)
 
         att = {}
         for jb in reversed(range(NB)):
@@ -130,7 +133,7 @@ def tile_flaxllamaattention_kernel(tc, tab, q, k, v, offs, out):
             seen = (jb + 1) * P
             att_t = psum_s.tile([P, N], BF16, name="att_t", tag="s_jt")
             for tb in range(jb + 1):
-                nc.tensor.transpose(att_t[:, block(tb)], att[jb][:, block(tb)], ident_bf[:])
+                nc.tensor.matmul(att_t[:, block(tb)], lhsT=att[jb][:, block(tb)], rhs=ident_bf[:], start=True, stop=True)
             att_tj = work.tile([P, N], BF16, name="att_tj")
             nc.vector.tensor_copy(att_tj[:, 0:seen], att_t[:, 0:seen])
             o_dj = psum_o.tile([P, P], F32, name="o_dj")

@@ -50,22 +50,22 @@ def tile_flaxllamaattention_kernel(tc, tab, q, k, v, offs, out):
         v_sb = held.tile([P, NB, P], BF16, name="v_sb")
         nc.sync.dma_start(v_sb[:], v.rearrange("(b t) d -> t b d", t=P))
 
-        ident_bf = held.tile([P, P], BF16, name="ident_bf")
-        make_identity(nc, ident_bf[:])
-        ident_f32 = held.tile([P, P], F32, name="ident_f32")
-        make_identity(nc, ident_f32[:])
         rotate = held.tile([P, P], F32, name="rotate")
         nc.gpsimd.memset(rotate[:], 0.0)
         for base, h_step, sign in ((-1, 2 * P, -1.0), (2 * P, -2 * P, 1.0)):
             nc.gpsimd.affine_select(out=rotate[:], in_=rotate[:], compare_op=NOT_EQUAL, fill=sign,
                                     base=base, pattern=[[-2, HALF], [h_step, 2]], channel_multiplier=1)
+        ident_f32 = held.tile([P, P], F32, name="ident_f32")
+        make_identity(nc, ident_f32[:])
+        ident_bf = held.tile([P, P], BF16, name="ident_bf")
+        make_identity(nc, ident_bf[:])
         mask_jt = held.tile([P, P], BF16, name="mask_jt")
         nc.gpsimd.memset(mask_jt[:], 0.0)
         nc.gpsimd.affine_select(out=mask_jt[:], in_=mask_jt[:], compare_op=IS_GE, fill=MASKED,
                                 base=0, pattern=[[-1, P]], channel_multiplier=1)
 
         warm_k = psum_o.tile([P, N], F32, name="warm_k", tag="o_dj")
-        nc.tensor.matmul(warm_k[:], lhsT=ident_f32[:], rhs=k_sb[:], start=True, stop=True)
+        nc.tensor.matmul(warm_k[:], lhsT=rotate[:], rhs=k_sb[:], start=True, stop=True)
 
         half = [slice(0, N // 2), slice(N // 2, N)]
         picks = [offsets[:, 0 : N // 32], offsets[:, N // 32 : N // 16]]
@@ -89,6 +89,8 @@ def tile_flaxllamaattention_kernel(tc, tab, q, k, v, offs, out):
             nc.vector.tensor_tensor(k_cos[:, half[h]], cos_tab[:].indirect(picks[h]), k_sb[:, half[h]], MULT)
         nc.tensor.matmul(kr_sum[:], lhsT=ident_f32[:], rhs=k_cos[:, half[0]], start=False, stop=True)
         nc.scalar.copy(kr[:, half[0]], kr_sum[:])
+        warm_cos = psum_o.tile([P, N // 2], F32, name="warm_cos", tag="o_dj")
+        nc.tensor.matmul(warm_cos[:], lhsT=ident_f32[:], rhs=k_cos[:, half[1]], start=True, stop=True)
         nc.vector.tensor_tensor(kr[:, half[1]], k_cos[:, half[1]], rk_sin[:], ADD)
         q_cos = held.tile([P, N], F32, name="q_cos")
         qr = held.tile([P, N], BF16, name="qr")

import math
from contextlib import ExitStack

import concourse.mybir as mybir
from concourse.masks import make_identity

F32 = mybir.dt.float32
BF16 = mybir.dt.bfloat16
U16 = mybir.dt.uint16
MULT = mybir.AluOpType.mult
ADD = mybir.AluOpType.add
MIN = mybir.AluOpType.min
NOT_EQUAL = mybir.AluOpType.not_equal
IS_GE = mybir.AluOpType.is_ge
EXP = mybir.ActivationFunctionType.Exp

P = 128
HALF = 64
S = 2048
N = 512
NB = N // P
SCALE = 1.0 / math.sqrt(P)
MASKED = -1.0e30

FLOPS = 2 * P * N * (N + 1)


def block(b):
    return slice(b * P, (b + 1) * P)


def tile_flaxllamaattention_kernel(tc, tab, q, k, v, offs, out):
    nc = tc.nc
    with ExitStack() as ctx:
        held = ctx.enter_context(tc.tile_pool(name="held", bufs=1))
        work = ctx.enter_context(tc.tile_pool(name="work", bufs=4))
        psum_s = ctx.enter_context(tc.psum_pool(name="psum_s", bufs=NB))
        psum_o = ctx.enter_context(tc.psum_pool(name="psum_o", bufs=NB))

        offsets = held.tile([P, N // 16], U16, name="offsets")
        nc.sync.dma_start(offsets[:], offs)
        k_sb = held.tile([P, N], F32, name="k_sb")
        sin_tab = held.tile([P, S], F32, name="sin_tab")
        q_sb = held.tile([P, N], F32, name="q_sb")
        cos_tab = held.tile([P, S], F32, name="cos_tab")
        sines, cosines = tab[0:P, :], tab[P : 2 * P, :]
        for tile, rows, lower_at in ((k_sb, k, 0), (sin_tab, sines, 1), (q_sb, q, 0), (cos_tab, cosines, 0)):
            nc.sync.dma_start(tile[lower_at:P:2, :], rows[0:HALF, :])
            nc.sync.dma_start(tile[1 - lower_at : P : 2, :], rows[HALF:P, :])
        v_sb = held.tile([P, NB, P], BF16, name="v_sb")
        nc.sync.dma_start(v_sb[:], v.rearrange("(b t) d -> t b d", t=P))

        rotate = held.tile([P, P], F32, name="rotate")
        nc.gpsimd.memset(rotate[:], 0.0)
        for base, h_step, sign in ((-1, 2 * P, -1.0), (2 * P, -2 * P, 1.0)):
            nc.gpsimd.affine_select(out=rotate[:], in_=rotate[:], compare_op=NOT_EQUAL, fill=sign,
                                    base=base, pattern=[[-2, HALF], [h_step, 2]], channel_multiplier=1)
        ident_f32 = held.tile([P, P], F32, name="ident_f32")
        make_identity(nc, ident_f32[:])
        ident_bf = held.tile([P, P], BF16, name="ident_bf")
        make_identity(nc, ident_bf[:])
        mask_jt = held.tile([P, P], BF16, name="mask_jt")
        nc.gpsimd.memset(mask_jt[:], 0.0)
        nc.gpsimd.affine_select(out=mask_jt[:], in_=mask_jt[:], compare_op=IS_GE, fill=MASKED,
                                base=0, pattern=[[-1, P]], channel_multiplier=1)

        warm_k = psum_o.tile([P, N], F32, name="warm_k", tag="o_dj")
        nc.tensor.matmul(warm_k[:], lhsT=rotate[:], rhs=k_sb[:], start=True, stop=True)

        half = [slice(0, N // 2), slice(N // 2, N)]
        picks = [offsets[:, 0 : N // 32], offsets[:, N // 32 : N // 16]]
        k_sin = held.tile([P, N], F32, name="k_sin")
        kr_sum = psum_o.tile([P, N // 2], F32, name="kr_sum", tag="o_dj")
        rk_sin = psum_o.tile([P, N // 2], F32, name="rk_sin", tag="o_dj")
        for h, rotated in ((0, kr_sum), (1, rk_sin)):
            nc.vector.tensor_tensor(k_sin[:, half[h]], sin_tab[:].indirect(picks[h]), k_sb[:, half[h]], MULT)
            nc.tensor.matmul(rotated[:], lhsT=rotate[:], rhs=k_sin[:, half[h]], start=True, stop=(h == 1))
        q_sin = held.tile([P, N], F32, name="q_sin")
        rq_sin = psum_o.tile([P, N], F32, name="rq_sin", tag="o_dj")
        for h in (1, 0):
            nc.vector.tensor_tensor(q_sin[:, half[h]], sin_tab[:].indirect(picks[h]), q_sb[:, half[h]], MULT)
            nc.tensor.matmul(rq_sin[:, half[h]], lhsT=rotate[:], rhs=q_sin[:, half[h]], start=True, stop=True)
        rq_sin_early = held.tile([P, N // 2], F32, name="rq_sin_early")
        nc.scalar.copy(rq_sin_early[:], rq_sin[:, half[0]])

        k_cos = held.tile([P, N], F32, name="k_cos")
        kr = held.tile([P, N], BF16, name="kr")
        for h in (0, 1):
            nc.vector.tensor_tensor(k_cos[:, half[h]], cos_tab[:].indirect(picks[h]), k_sb[:, half[h]], MULT)
        nc.tensor.matmul(kr_sum[:], lhsT=ident_f32[:], rhs=k_cos[:, half[0]], start=False, stop=True)
        nc.scalar.copy(kr[:, half[0]], kr_sum[:])
        warm_cos = psum_o.tile([P, N // 2], F32, name="warm_cos", tag="o_dj")
        nc.tensor.matmul(warm_cos[:], lhsT=ident_f32[:], rhs=k_cos[:, half[1]], start=True, stop=True)
        nc.vector.tensor_tensor(kr[:, half[1]], k_cos[:, half[1]], rk_sin[:], ADD)
        q_cos = held.tile([P, N], F32, name="q_cos")
        qr = held.tile([P, N], BF16, name="qr")
        for jb in reversed(range(NB)):
            picked = cos_tab[:].indirect(offsets[:, jb * (P // 16) : (jb + 1) * (P // 16)])
            nc.vector.tensor_tensor(q_cos[:, block(jb)], picked, q_sb[:, block(jb)], MULT)
            adder, rotated = (nc.vector, rq_sin) if jb >= NB // 2 else (nc.gpsimd, rq_sin_early)
            adder.tensor_tensor(qr[:, block(jb)], q_cos[:, block(jb)], rotated[:, block(jb)], ADD)

        att = {}
        for jb in reversed(range(NB)):
            seen = (jb + 1) * P

            s_jt = psum_s.tile([P, N], F32, name="s_jt")
            nc.tensor.matmul(s_jt[:, block(jb)], lhsT=ident_bf[:], rhs=mask_jt[:],
                             start=True, stop=False)
            if jb > 0:
                nc.tensor.matmul(s_jt[:, 0 : jb * P], lhsT=qr[:, block(jb)], rhs=kr[:, 0 : jb * P],
                                 start=False, stop=False)
            nc.tensor.matmul(s_jt[:, block(jb)], lhsT=qr[:, block(jb)], rhs=kr[:, block(jb)],
                             start=False, stop=True)

            neg_s = work.tile([P, N], F32, name="neg_s")
            bias = work.tile([P, 1], F32, name="bias")
            nc.vector.tensor_scalar(out=neg_s[:, 0:seen], in0=s_jt[:, 0:seen], scalar1=-SCALE, scalar2=None,
                                    op0=MULT, op1=MIN, accum_out=bias[:])
            if jb == NB - 1:
                warm = psum_o.tile([P, N // 2], F32, name="warm", tag="o_dj")
                nc.tensor.matmul(warm[:], lhsT=rotate[:], rhs=neg_s[:, 0 : N // 2], start=True, stop=True)
            e_jt = work.tile([P, N], F32, name="e_jt")
            e_sum = work.tile([P, 1], F32, name="e_sum")
            nc.scalar.activation(e_jt[:, 0:seen], neg_s[:, 0:seen], EXP, bias=bias[:], scale=-1.0,
                                 accum_out=e_sum[:])
            r_sum = work.tile([P, 1], F32, name="r_sum")
            nc.vector.reciprocal(r_sum[:], e_sum[:])
            att[jb] = work.tile([P, N], BF16, name="att")
            nc.vector.tensor_scalar(out=att[jb][:, 0:seen], in0=e_jt[:, 0:seen], scalar1=r_sum[:, 0:1], scalar2=None,
                                    op0=MULT)

        out_sb = held.tile([P, N], F32, name="out_sb")
        for jb in reversed(range(NB)):
            seen = (jb + 1) * P
            att_t = psum_s.tile([P, N], BF16, name="att_t", tag="s_jt")
            for tb in range(jb + 1):
                nc.tensor.matmul(att_t[:, block(tb)], lhsT=att[jb][:, block(tb)], rhs=ident_bf[:], start=True, stop=True)
            att_tj = work.tile([P, N], BF16, name="att_tj")
            nc.vector.tensor_copy(att_tj[:, 0:seen], att_t[:, 0:seen])
            o_dj = psum_o.tile([P, P], F32, name="o_dj")
            for tb in range(jb + 1):
                nc.tensor.matmul(o_dj[:], lhsT=v_sb[:, tb, :], rhs=att_tj[:, block(tb)],
                                 start=(tb == 0), stop=(tb == jb))
            nc.scalar.copy(out_sb[:, block(jb)], o_dj[:])
            nc.sync.dma_start(out[:, block(jb)], out_sb[:, block(jb)])
